import numpy as np
import ml_dtypes


def mxq(x, axis, fmt="e4m3"):
    dtype, down = {"e4m3": (ml_dtypes.float8_e4m3fn, 7), "e5m2": (ml_dtypes.float8_e5m2, 14)}[fmt]
    v = np.moveaxis(np.asarray(x, np.float32).astype(ml_dtypes.bfloat16).astype(np.float64), axis, -1)
    blocks = v.reshape(v.shape[:-1] + (-1, 32))
    amax = np.abs(blocks).max(-1, keepdims=True)
    byte = np.maximum(np.where(amax > 0, np.frexp(amax)[1] - 1 + 127, 0) - down, 1)
    scale = np.exp2(byte - 127.0)
    codes = (blocks / scale).astype(np.float32).astype(dtype).astype(np.float64)
    return np.moveaxis((codes * scale).reshape(v.shape), -1, axis)


WIDE = False


def mx_kscale(k):
    if not WIDE:
        return np.ones(k)
    levels = np.array([10, -10, 5, -5, 0])
    if k % 512:
        return np.exp2(np.random.permutation(np.resize(levels, k // 32))).repeat(32)
    a = np.empty((k // 512, 16))
    for p in range(k // 512):
        a[p, :8] = np.random.permutation(np.resize(levels, 8))
        for g in range(8):
            far = levels[np.abs(levels - a[p, g]) >= 10]
            a[p, g + 8] = far[np.random.randint(len(far))]
    return np.exp2(a.ravel()).repeat(32)


BF16 = ml_dtypes.bfloat16


def bf(x):
    return np.asarray(x, np.float32).astype(BF16)


def f64(x):
    return np.asarray(x).astype(np.float64)


B, N, D = 32, 256, 512


def setup_inputs():
    s = mx_kscale(D)
    return {"panel_embeddings": bf(np.random.standard_normal((B, N, D)) * s),
            "W": bf(np.random.standard_normal((D, D)) * 4.0 / D / s[:, None] / s[None, :]),
            "b": bf(0.5 + 0.1 * np.random.standard_normal(1))}


def reference(panel_embeddings, W, b):
    xq = mxq(f64(panel_embeddings), 2, "e4m3")
    xw = xq @ mxq(f64(W), 0, "e4m3")
    scores = (mxq(xw, 2, "e4m3") @ xq.transpose(0, 2, 1)) + f64(b)
    n = panel_embeddings.shape[1]
    mask = ~np.eye(n, dtype=bool)
    return np.where(mask, scores, np.zeros_like(scores))

@@ -1,0 +1,287 @@
+from contextlib import ExitStack
+
+import concourse.mybir as mybir
+from concourse.masks import make_identity
+
+F32 = mybir.dt.float32
+BF16 = mybir.dt.bfloat16
+U32 = mybir.dt.uint32
+U8 = mybir.dt.uint8
+FP8X4 = mybir.dt.float8_e4m3fn_x4
+ADD = mybir.AluOpType.add
+MULT = mybir.AluOpType.mult
+
+P = 128
+B, N, D = 32, 256, 512
+FLOPS = 2 * B * N * D * D + 2 * B * N * N * D
+NC = B // 2
+MANUAL = True
+LOADS_AHEAD = 10
+
+
+def cx_on_vector(b):
+    return b == 3
+
+
+def cw_on_vector(c, g):
+    if c < 2:
+        return g in (1, 3)
+    return c < 14 and g == 1 and c % 6 != 0
+
+
+def tile_readingorderhead_t_kernel(tc, panel_embeddings, W, b, out):
+    nc = tc.nc
+    x = panel_embeddings
+    with ExitStack() as ctx:
+        const = ctx.enter_context(tc.tile_pool(name="const", bufs=1))
+        xin = ctx.enter_context(tc.tile_pool(name="xin", bufs=1))
+        work = ctx.enter_context(tc.tile_pool(name="work", bufs=4))
+        outp = ctx.enter_context(tc.tile_pool(name="outp", bufs=8))
+        psum = ctx.enter_context(tc.psum_pool(name="psum", bufs=2))
+        if MANUAL:
+            ctx.enter_context(tc.manual_schedule())
+
+        x_of = {}
+
+        def load_x(b0, nb):
+            xr = xin.tile([P, nb * 2 * D], BF16, name="x_raw%d" % b0)
+            nc.sync.dma_start(
+                out=xr[:].rearrange("p (b f) -> p b f", b=nb),
+                in_=x[b0 : b0 + nb].rearrange("b (p r) d -> p b (r d)", r=2),
+            )
+            for j in range(nb):
+                x_of[b0 + j] = (xr, j)
+
+        load_x(0, 1)
+        w_raw = const.tile([P, 4, D], BF16, name="w_raw")
+        nc.sync.dma_start(
+            out=w_raw[:].rearrange("p t n -> p (t n)"),
+            in_=W.rearrange("(p t) n -> p (t n)", t=4),
+        )
+        load_x(1, 1)
+        b_row = const.tile([P, 32], BF16, name="b_row")
+        nc.vector.memset(b_row[:], 0.0)
+        nc.scalar.dma_start(out=b_row[0:1, 0:1], in_=b.unsqueeze(0))
+        ones = const.tile([P, P], BF16, name="ones")
+        nc.vector.memset(ones[:], 1.0)
+        for c in range(1, LOADS_AHEAD):
+            load_x(2 * c, 2)
+
+        ident = const.tile([P, P], F32, name="ident")
+        make_identity(nc, ident[:])
+        mask = const.tile([P, 2 * N], F32, name="mask")
+        nc.vector.memset(mask[:], 1.0)
+        mask_v = mask[:].rearrange("p (r q s) -> p r q s", r=2, q=P, s=2)
+        for r in range(2):
+            nc.vector.tensor_scalar(
+                out=mask_v[:, r, :, r], in0=ident[:], scalar1=-1.0, scalar2=1.0, op0=MULT, op1=ADD
+            )
+        bias = const.tile([P, 1], F32, name="bias")
+
+        wg = const.tile([P, 4 * D], BF16, name="wg", align_bytes=64)
+        wc = const.tile([P, D], U32, name="wc", align_bytes=64)
+        ws = const.tile([P, D], U8, name="ws", align_bytes=64)
+
+        def w_regroup():
+            wg_v = wg[:].rearrange("p (o m t) -> p o m t", o=4, m=P, t=4)
+            w_v = w_raw[:].rearrange("p t (m o) -> p o m t", m=P, o=4)
+            for o in range(4):
+                src = w_v[:, o, :, :]
+                if o == 3:
+                    nc.scalar.copy(out=wg_v[:, o, :, :], in_=src)
+                else:
+                    nc.vector.tensor_copy(out=wg_v[:, o, :, :], in_=src)
+
+        def w_quantise():
+            nc.vector.quantize_mx(out=wc[:].bitcast(FP8X4), scales=ws[:], in_=wg[:])
+            nc.vector.tensor_copy(out=bias[:], in_=bias_ps[0][:, 0:1])
+
+        xt_t, xg_of, xc_of, xw_t, xwg_of, xwc_of, sc_t, o_of = {}, {}, {}, {}, {}, {}, {}, {}
+
+        def ok(c):
+            return 0 <= c < NC
+
+        def copy_out(on_vector, dst, src):
+            if on_vector:
+                nc.vector.tensor_copy(out=dst, in_=src)
+            else:
+                nc.scalar.copy(out=dst, in_=src)
+
+        bias_ps = []
+
+        def spread_bias():
+            bp = psum.tile([P, 32], F32, name="bp", tag="sc", bufs=2)
+            nc.tensor.matmul(out=bp[:], lhsT=ones[:], rhs=b_row[:], start=True, stop=True)
+            bias_ps.append(bp)
+
+        def tr(c):
+            if not ok(c):
+                return
+            for bb in (2 * c, 2 * c + 1):
+                if bb == 1:
+                    spread_bias()
+                xr, j = x_of[bb]
+                xr32 = xr[:].bitcast(F32)
+                xt = psum.tile([P, 4, P], F32, name="xt", tag="xt", bufs=2)
+                for s in range(4):
+                    lo = 512 * j + 256 * (s // 2)
+                    nc.tensor.transpose(xt[:, s, :], xr32[:, lo + s % 2 : lo + 256 : 2], ident[:])
+                xt_t[bb] = xt
+
+        def cx(c, j):
+            if not ok(c):
+                return
+            bb = 2 * c + j
+            if c == 0:
+                xg = work.tile([P, 4 * N], BF16, name="xg", tag="xg", align_bytes=64)
+                xg_of[bb] = (xg, 0)
+            elif j == 0:
+                xg = work.tile([P, 8 * N], BF16, name="xg", tag="xg", align_bytes=64)
+                xg_of[bb] = (xg, 0)
+                xg_of[bb + 1] = (xg, 1)
+            xg, k = xg_of[bb]
+            dst = xg[:].bitcast(F32)[:, 512 * k : 512 * (k + 1)].rearrange("q (p s) -> q p s", s=4)
+            copy_out(cx_on_vector(bb), dst, xt_t[bb][:].rearrange("q s p -> q p s"))
+
+        def quantise(src, nb, tag, bufs):
+            cod = work.tile([P, nb * N], U32, name=tag + "c", tag=tag + "c", bufs=bufs, align_bytes=64)
+            sca = work.tile([P, nb * N], U8, name=tag + "s", tag=tag + "s", bufs=bufs, align_bytes=64)
+            nc.vector.quantize_mx(out=cod[:].bitcast(FP8X4), scales=sca[:], in_=src[:])
+            return cod, sca
+
+        def qx(c):
+            if not ok(c):
+                return
+            if c == 0:
+                for bb in (0, 1):
+                    cod, sca = quantise(xg_of[bb][0], 1, "xq", 7)
+                    xc_of[bb] = (cod, sca, 0)
+            else:
+                cod, sca = quantise(xg_of[2 * c][0], 2, "xq", 7)
+                xc_of[2 * c] = (cod, sca, 0)
+                xc_of[2 * c + 1] = (cod, sca, 1)
+
+        def s1(c, g):
+            if not ok(c):
+                return
+            cod, sca, k = xc_of[2 * c + g // 2]
+            lo = N * k + P * (g % 2)
+            xw = psum.tile([P, 4, P], F32, name="xw", tag="xw", bufs=4)
+            for t in range(4):
+                nc.tensor.matmul_mx(
+                    out=xw[:, t, :],
+                    lhsT=wc[:, P * t : P * (t + 1)].bitcast(FP8X4),
+                    lhsT_scale=ws[:, P * t : P * (t + 1)],
+                    rhs=cod[:, lo : lo + P].bitcast(FP8X4),
+                    rhs_scale=sca[:, lo : lo + P],
+                    start=True,
+                    stop=True,
+                )
+            xw_t[(c, g)] = xw
+
+        def cw(c, g):
+            if not ok(c):
+                return
+            bb, a = 2 * c + g // 2, g % 2
+            if c == NC - 1:
+                if a == 0:
+                    xwg = work.tile([P, 4 * N], BF16, name="xwg", tag="xwg", align_bytes=64)
+                    xwg_of[bb] = (xwg, 0, 1)
+            elif g == 0:
+                xwg = work.tile([P, 8 * N], BF16, name="xwg", tag="xwg", align_bytes=64)
+                xwg_of[bb] = (xwg, 0, 2)
+                xwg_of[bb + 1] = (xwg, 1, 2)
+            xwg, k, nb = xwg_of[bb]
+            xwg_v = xwg[:].rearrange("p (b r m t) -> p b r m t", b=nb, r=2, m=P, t=4)
+            dst = xwg_v[:, k, :, 64 * a : 64 * (a + 1), :]
+            copy_out(cw_on_vector(c, g), dst, xw_t[(c, g)][:].rearrange("p t (m r) -> p r m t", r=2))
+
+        def qw_batch(bb):
+            cod, sca = quantise(xwg_of[bb][0], 1, "wq", 4)
+            xwc_of[bb] = (cod, sca, 0)
+
+        def qw(c):
+            if not ok(c):
+                return
+            cod, sca = quantise(xwg_of[2 * c][0], 2, "wq", 4)
+            xwc_of[2 * c] = (cod, sca, 0)
+            xwc_of[2 * c + 1] = (cod, sca, 1)
+
+        def s2(c):
+            if not ok(c):
+                return
+            for bb in (2 * c, 2 * c + 1):
+                xcod, xsca, k = xc_of[bb]
+                wcod, wsca, kw = xwc_of[bb]
+                sc = psum.tile([P, 2, N], F32, name="sc", tag="sc", bufs=2)
+                for r in range(2):
+                    lo = N * kw + P * r
+                    nc.tensor.matmul_mx(
+                        out=sc[:, r, :],
+                        lhsT=wcod[:, lo : lo + P].bitcast(FP8X4),
+                        lhsT_scale=wsca[:, lo : lo + P],
+                        rhs=xcod[:, N * k : N * (k + 1)].bitcast(FP8X4),
+                        rhs_scale=xsca[:, N * k : N * (k + 1)],
+                        start=True,
+                        stop=True,
+                    )
+                sc_t[bb] = sc
+
+        def store(b0, nb, o):
+            nc.sync.dma_start(
+                out=out[b0 : b0 + nb].rearrange("b (p r) j -> p b (r j)", r=2), in_=o[:]
+            )
+
+        def ex(c, j):
+            if not ok(c):
+                return
+            bb = 2 * c + j
+            if c == NC - 1:
+                o = outp.tile([P, 1, 2 * N], F32, name="o", tag="o")
+                o_of[bb] = (o, 0)
+            elif j == 0:
+                o = outp.tile([P, 2, 2 * N], F32, name="o", tag="o")
+                o_of[bb] = (o, 0)
+                o_of[bb + 1] = (o, 1)
+            o, k = o_of[bb]
+            nc.vector.scalar_tensor_tensor(
+                out=o[:, k, :],
+                in0=sc_t[bb][:].rearrange("p r j -> p (r j)"),
+                scalar=bias[:, 0:1],
+                in1=mask[:],
+                op0=ADD,
+                op1=MULT,
+            )
+            if c == NC - 1:
+                store(bb, 1, o)
+            elif j == 1:
+                store(bb - 1, 2, o)
+                if c + LOADS_AHEAD < NC:
+                    load_x(2 * (c + LOADS_AHEAD), 2)
+
+        for i in range(-2, NC + 3):
+            s1(i, 0)
+            cw(i - 1, 3)
+            s1(i, 1)
+            if i == -1:
+                w_regroup()
+            cx(i + 1, 0)
+            s1(i, 2)
+            cx(i + 1, 1)
+            s1(i, 3)
+            if i - 1 == NC - 1:
+                qw_batch(B - 2)
+                ex(i - 2, 0)
+                qw_batch(B - 1)
+            else:
+                ex(i - 2, 0)
+                qw(i - 1)
+            ex(i - 2, 1)
+            if i == -1:
+                w_quantise()
+            tr(i + 2)
+            cw(i, 0)
+            s2(i - 1)
+            qx(i + 1)
+            cw(i, 1)
+            cw(i, 2)

@@ -10,6 +10,8 @@ U8 = mybir.dt.uint8
 FP8X4 = mybir.dt.float8_e4m3fn_x4
 ADD = mybir.AluOpType.add
 MULT = mybir.AluOpType.mult
+IDENTITY = mybir.ActivationFunctionType.Identity
+SPLIT_FROM = 14
 
 P = 128
 B, N, D = 32, 256, 512
@@ -17,16 +19,6 @@ FLOPS = 2 * B * N * D * D + 2 * B * N * N * D
 NC = B // 2
 MANUAL = True
 LOADS_AHEAD = 10
-
-
-def cx_on_vector(b):
-    return b == 3
-
-
-def cw_on_vector(c, g):
-    if c < 2:
-        return g in (1, 3)
-    return c < 14 and g == 1 and c % 6 != 0
 
 
 def tile_readingorderhead_t_kernel(tc, panel_embeddings, W, b, out):
@@ -64,6 +56,8 @@ def tile_readingorderhead_t_kernel(tc, panel_embeddings, W, b, out):
         nc.scalar.dma_start(out=b_row[0:1, 0:1], in_=b.unsqueeze(0))
         ones = const.tile([P, P], BF16, name="ones")
         nc.vector.memset(ones[:], 1.0)
+        zeros = const.tile([P, 512], BF16, name="zeros")
+        nc.vector.memset(zeros[:], 0.0)
         for c in range(1, LOADS_AHEAD):
             load_x(2 * c, 2)
 
@@ -75,6 +69,11 @@ def tile_readingorderhead_t_kernel(tc, panel_embeddings, W, b, out):
         for r in range(2):
             nc.vector.tensor_scalar(
                 out=mask_v[:, r, :, r], in0=ident[:], scalar1=-1.0, scalar2=1.0, op0=MULT, op1=ADD
+            )
+        dmask = const.tile([P, 2 * P], F32, name="dmask")
+        for r in range(2):
+            nc.vector.tensor_scalar(
+                out=dmask[:, P * r : P * (r + 1)], in0=ident[:], scalar1=-1.0, scalar2=1.0, op0=MULT, op1=ADD
             )
         bias = const.tile([P, 1], F32, name="bias")
 
@@ -114,21 +113,26 @@ def tile_readingorderhead_t_kernel(tc, panel_embeddings, W, b, out):
             nc.tensor.matmul(out=bp[:], lhsT=ones[:], rhs=b_row[:], start=True, stop=True)
             bias_ps.append(bp)
 
-        def tr(c):
-            if not ok(c):
-                return
-            for bb in (2 * c, 2 * c + 1):
-                if bb == 1:
-                    spread_bias()
-                xr, j = x_of[bb]
-                xr32 = xr[:].bitcast(F32)
-                xt = psum.tile([P, 4, P], F32, name="xt", tag="xt", bufs=2)
-                for s in range(4):
-                    lo = 512 * j + 256 * (s // 2)
-                    nc.tensor.transpose(xt[:, s, :], xr32[:, lo + s % 2 : lo + 256 : 2], ident[:])
-                xt_t[bb] = xt
+        def warm(n):
+            wp = psum.tile([P, 512], F32, name="wp", tag="xw", bufs=4)
+            for k in range(n):
+                nc.tensor.matmul(out=wp[:], lhsT=ones[:], rhs=zeros[:], start=True, stop=True)
 
-        def cx(c, j):
+        def tr_batch(bb):
+            xr, j = x_of[bb]
+            xr32 = xr[:].bitcast(F32)
+            xt = psum.tile([P, 4, P], F32, name="xt", tag="xt", bufs=2)
+            for s in range(4):
+                lo = 512 * j + 256 * (s // 2)
+                nc.tensor.transpose(xt[:, s, :], xr32[:, lo + s % 2 : lo + 256 : 2], ident[:])
+            xt_t[bb] = xt
+
+        def tr(c):
+            if ok(c):
+                tr_batch(2 * c)
+                tr_batch(2 * c + 1)
+
+        def cx(c, j, on_vector=False):
             if not ok(c):
                 return
             bb = 2 * c + j
@@ -141,7 +145,7 @@ def tile_readingorderhead_t_kernel(tc, panel_embeddings, W, b, out):
                 xg_of[bb + 1] = (xg, 1)
             xg, k = xg_of[bb]
             dst = xg[:].bitcast(F32)[:, 512 * k : 512 * (k + 1)].rearrange("q (p s) -> q p s", s=4)
-            copy_out(cx_on_vector(bb), dst, xt_t[bb][:].rearrange("q s p -> q p s"))
+            copy_out(on_vector, dst, xt_t[bb][:].rearrange("q s p -> q p s"))
 
         def quantise(src, nb, tag, bufs):
             cod = work.tile([P, nb * N], U32, name=tag + "c", tag=tag + "c", bufs=bufs, align_bytes=64)
@@ -149,14 +153,12 @@ def tile_readingorderhead_t_kernel(tc, panel_embeddings, W, b, out):
             nc.vector.quantize_mx(out=cod[:].bitcast(FP8X4), scales=sca[:], in_=src[:])
             return cod, sca
 
+        def qx_batch(bb):
+            cod, sca = quantise(xg_of[bb][0], 1, "xq", 7)
+            xc_of[bb] = (cod, sca, 0)
+
         def qx(c):
-            if not ok(c):
-                return
-            if c == 0:
-                for bb in (0, 1):
-                    cod, sca = quantise(xg_of[bb][0], 1, "xq", 7)
-                    xc_of[bb] = (cod, sca, 0)
-            else:
+            if ok(c):
                 cod, sca = quantise(xg_of[2 * c][0], 2, "xq", 7)
                 xc_of[2 * c] = (cod, sca, 0)
                 xc_of[2 * c + 1] = (cod, sca, 1)
@@ -179,7 +181,7 @@ def tile_readingorderhead_t_kernel(tc, panel_embeddings, W, b, out):
                 )
             xw_t[(c, g)] = xw
 
-        def cw(c, g):
+        def cw(c, g, on_vector=False):
             if not ok(c):
                 return
             bb, a = 2 * c + g // 2, g % 2
@@ -193,8 +195,13 @@ def tile_readingorderhead_t_kernel(tc, panel_embeddings, W, b, out):
                 xwg_of[bb + 1] = (xwg, 1, 2)
             xwg, k, nb = xwg_of[bb]
             xwg_v = xwg[:].rearrange("p (b r m t) -> p b r m t", b=nb, r=2, m=P, t=4)
-            dst = xwg_v[:, k, :, 64 * a : 64 * (a + 1), :]
-            copy_out(cw_on_vector(c, g), dst, xw_t[(c, g)][:].rearrange("p t (m r) -> p r m t", r=2))
+            if c >= SPLIT_FROM:
+                dst = xwg[:].rearrange("p (n t) -> p n t", t=4)[:, N * k + P * a : N * k + P * (a + 1), :]
+                src = xw_t[(c, g)][:].rearrange("p t n -> p n t")
+            else:
+                dst = xwg_v[:, k, :, 64 * a : 64 * (a + 1), :]
+                src = xw_t[(c, g)][:].rearrange("p t (m r) -> p r m t", r=2)
+            copy_out(on_vector, dst, src)
 
         def qw_batch(bb):
             cod, sca = quantise(xwg_of[bb][0], 1, "wq", 4)
@@ -214,6 +221,26 @@ def tile_readingorderhead_t_kernel(tc, panel_embeddings, W, b, out):
                 xcod, xsca, k = xc_of[bb]
                 wcod, wsca, kw = xwc_of[bb]
                 sc = psum.tile([P, 2, N], F32, name="sc", tag="sc", bufs=2)
+                if c >= SPLIT_FROM:
+                    if c == NC - 1:
+                        off = psum.tile([P, 4, P], F32, name="off", tag="xw", bufs=4)
+                    else:
+                        off = psum.tile([P, 4, P], F32, name="off", tag="xt", bufs=2)
+                    for r in range(2):
+                        lo = N * kw + P * r
+                        for h in range(2):
+                            hi = N * k + P * h
+                            nc.tensor.matmul_mx(
+                                out=(sc[:, 0, P * r : P * (r + 1)] if h == r else off[:, r, :]),
+                                lhsT=wcod[:, lo : lo + P].bitcast(FP8X4),
+                                lhsT_scale=wsca[:, lo : lo + P],
+                                rhs=xcod[:, hi : hi + P].bitcast(FP8X4),
+                                rhs_scale=xsca[:, hi : hi + P],
+                                start=True,
+                                stop=True,
+                            )
+                    sc_t[bb] = (sc, off)
+                    continue
                 for r in range(2):
                     lo = N * kw + P * r
                     nc.tensor.matmul_mx(
@@ -227,7 +254,14 @@ def tile_readingorderhead_t_kernel(tc, panel_embeddings, W, b, out):
                     )
                 sc_t[bb] = sc
 
-        def store(b0, nb, o):
+        def store(b0, nb, o, blocks=False):
+            if blocks:
+                for b in range(nb):
+                    nc.sync.dma_start(
+                        out=out[b0 + b].rearrange("(r p) j -> p r j", r=2),
+                        in_=o[:, b, :].rearrange("p (r j) -> p r j", r=2),
+                    )
+                return
             nc.sync.dma_start(
                 out=out[b0 : b0 + nb].rearrange("b (p r) j -> p b (r j)", r=2), in_=o[:]
             )
@@ -244,6 +278,25 @@ def tile_readingorderhead_t_kernel(tc, panel_embeddings, W, b, out):
                 o_of[bb] = (o, 0)
                 o_of[bb + 1] = (o, 1)
             o, k = o_of[bb]
+            if c >= SPLIT_FROM:
+                sc, off = sc_t[bb]
+                o4 = o[:, k, :].rearrange("p (g j) -> p g j", g=4)
+                nc.vector.scalar_tensor_tensor(
+                    out=o4[:, 0:4:3, :],
+                    in0=sc[:, 0, :].rearrange("p (r j) -> p r j", r=2),
+                    scalar=bias[:, 0:1],
+                    in1=dmask[:].rearrange("p (r j) -> p r j", r=2),
+                    op0=ADD,
+                    op1=MULT,
+                )
+                nc.scalar.activation(
+                    out=o4[:, 1:3, :], in_=off[:, 0:2, :], func=IDENTITY, bias=bias[:, 0:1]
+                )
+                if c == NC - 1:
+                    store(bb, 1, o, True)
+                elif j == 1:
+                    store(bb - 1, 2, o, True)
+                return
             nc.vector.scalar_tensor_tensor(
                 out=o[:, k, :],
                 in0=sc_t[bb][:].rearrange("p r j -> p (r j)"),
@@ -259,29 +312,50 @@ def tile_readingorderhead_t_kernel(tc, panel_embeddings, W, b, out):
                 if c + LOADS_AHEAD < NC:
                     load_x(2 * (c + LOADS_AHEAD), 2)
 
-        for i in range(-2, NC + 3):
+        warm(3)
+        tr_batch(0)
+        warm(2)
+        cx(0, 0)
+        w_regroup()
+        spread_bias()
+        tr_batch(1)
+        warm(1)
+        qx_batch(0)
+        w_quantise()
+        cx(0, 1)
+        qx_batch(1)
+        tr_batch(2)
+        s1(0, 0)
+        s1(0, 1)
+        cx(1, 0)
+        cw(0, 0, True)
+        tr_batch(3)
+        cw(0, 1)
+        s1(0, 2)
+        s1(0, 3)
+        cx(1, 1, True)
+        tr(2)
+        qx(1)
+        cw(0, 2)
+        for i in range(1, NC + 2):
             s1(i, 0)
-            cw(i - 1, 3)
+            cw(i - 1, 3, i==2)
             s1(i, 1)
-            if i == -1:
-                w_regroup()
             cx(i + 1, 0)
             s1(i, 2)
-            cx(i + 1, 1)
             s1(i, 3)
-            if i - 1 == NC - 1:
+            if i == NC:
                 qw_batch(B - 2)
                 ex(i - 2, 0)
                 qw_batch(B - 1)
             else:
                 ex(i - 2, 0)
                 qw(i - 1)
+            cx(i + 1, 1, i == 1)
             ex(i - 2, 1)
-            if i == -1:
-                w_quantise()
             tr(i + 2)
             cw(i, 0)
             s2(i - 1)
             qx(i + 1)
-            cw(i, 1)
+            cw(i, 1, 1 < i < 14 and i % 6 != 0)
             cw(i, 2)

@@ -19,6 +19,8 @@ FLOPS = 2 * B * N * D * D + 2 * B * N * N * D
 NC = B // 2
 MANUAL = True
 LOADS_AHEAD = 10
+XQ_BUFS = 16
+WQ_BUFS = 16
 
 
 def tile_readingorderhead_t_kernel(tc, panel_embeddings, W, b, out):
@@ -27,8 +29,8 @@ def tile_readingorderhead_t_kernel(tc, panel_embeddings, W, b, out):
     with ExitStack() as ctx:
         const = ctx.enter_context(tc.tile_pool(name="const", bufs=1))
         xin = ctx.enter_context(tc.tile_pool(name="xin", bufs=1))
-        work = ctx.enter_context(tc.tile_pool(name="work", bufs=4))
-        outp = ctx.enter_context(tc.tile_pool(name="outp", bufs=8))
+        work = ctx.enter_context(tc.tile_pool(name="work", bufs=3))
+        outp = ctx.enter_context(tc.tile_pool(name="outp", bufs=16))
         psum = ctx.enter_context(tc.psum_pool(name="psum", bufs=2))
         if MANUAL:
             ctx.enter_context(tc.manual_schedule())
@@ -36,7 +38,10 @@ def tile_readingorderhead_t_kernel(tc, panel_embeddings, W, b, out):
         x_of = {}
 
         def load_x(b0, nb):
-            xr = xin.tile([P, nb * 2 * D], BF16, name="x_raw%d" % b0)
+            if nb == 1:
+                xr = xin.tile([P, 2 * D], BF16, name="x_raw%d" % b0)
+            else:
+                xr = xin.tile([P, 4 * D], BF16, name="x_raw", tag="x_raw", bufs=LOADS_AHEAD)
             nc.sync.dma_start(
                 out=xr[:].rearrange("p (b f) -> p b f", b=nb),
                 in_=x[b0 : b0 + nb].rearrange("b (p r) d -> p b (r d)", r=2),
@@ -154,12 +159,12 @@ def tile_readingorderhead_t_kernel(tc, panel_embeddings, W, b, out):
             return cod, sca
 
         def qx_batch(bb):
-            cod, sca = quantise(xg_of[bb][0], 1, "xq", 7)
+            cod, sca = quantise(xg_of[bb][0], 1, "xq", XQ_BUFS)
             xc_of[bb] = (cod, sca, 0)
 
         def qx(c):
             if ok(c):
-                cod, sca = quantise(xg_of[2 * c][0], 2, "xq", 7)
+                cod, sca = quantise(xg_of[2 * c][0], 2, "xq", XQ_BUFS)
                 xc_of[2 * c] = (cod, sca, 0)
                 xc_of[2 * c + 1] = (cod, sca, 1)
 
@@ -204,13 +209,13 @@ def tile_readingorderhead_t_kernel(tc, panel_embeddings, W, b, out):
             copy_out(on_vector, dst, src)
 
         def qw_batch(bb):
-            cod, sca = quantise(xwg_of[bb][0], 1, "wq", 4)
+            cod, sca = quantise(xwg_of[bb][0], 1, "wq", WQ_BUFS)
             xwc_of[bb] = (cod, sca, 0)
 
         def qw(c):
             if not ok(c):
                 return
-            cod, sca = quantise(xwg_of[2 * c][0], 2, "wq", 4)
+            cod, sca = quantise(xwg_of[2 * c][0], 2, "wq", WQ_BUFS)
             xwc_of[2 * c] = (cod, sca, 0)
             xwc_of[2 * c + 1] = (cod, sca, 1)
 
@@ -218,6 +223,8 @@ def tile_readingorderhead_t_kernel(tc, panel_embeddings, W, b, out):
             if not ok(c):
                 return
             for bb in (2 * c, 2 * c + 1):
+                if bb == B - 1:
+                    continue
                 xcod, xsca, k = xc_of[bb]
                 wcod, wsca, kw = xwc_of[bb]
                 sc = psum.tile([P, 2, N], F32, name="sc", tag="sc", bufs=2)
@@ -254,16 +261,57 @@ def tile_readingorderhead_t_kernel(tc, panel_embeddings, W, b, out):
                     )
                 sc_t[bb] = sc
 
-        def store(b0, nb, o, blocks=False):
-            if blocks:
-                for b in range(nb):
-                    nc.sync.dma_start(
-                        out=out[b0 + b].rearrange("(r p) j -> p r j", r=2),
-                        in_=o[:, b, :].rearrange("p (r j) -> p r j", r=2),
-                    )
-                return
+        def qw_half(a):
+            cod = work.tile([P, P], U32, name="whc", tag="whc", bufs=2, align_bytes=64)
+            sca = work.tile([P, P], U8, name="whs", tag="whs", bufs=2, align_bytes=64)
+            xwg = xwg_of[B - 1][0]
+            nc.vector.quantize_mx(
+                out=cod[:].bitcast(FP8X4), scales=sca[:], in_=xwg[:, 4 * P * a : 4 * P * (a + 1)]
+            )
+            xwc_of[(B - 1, a)] = (cod, sca)
+
+        def s2_half(r):
+            xcod, xsca, k = xc_of[B - 1]
+            wcod, wsca = xwc_of[(B - 1, r)]
+            if r == 0:
+                sc = psum.tile([P, P], F32, name="sch0", tag="sc", bufs=2)
+                off = psum.tile([P, P], F32, name="offh0", tag="xt", bufs=2)
+            else:
+                sc = psum.tile([P, P], F32, name="sch1", tag="xw", bufs=4)
+                off = psum.tile([P, P], F32, name="offh1", tag="xw", bufs=4)
+            for h in range(2):
+                hi = N * k + P * h
+                nc.tensor.matmul_mx(
+                    out=sc[:] if h == r else off[:],
+                    lhsT=wcod[:].bitcast(FP8X4),
+                    lhsT_scale=wsca[:],
+                    rhs=xcod[:, hi : hi + P].bitcast(FP8X4),
+                    rhs_scale=xsca[:, hi : hi + P],
+                    start=True,
+                    stop=True,
+                )
+            sc_t[(B - 1, r)] = (sc, off)
+
+        def ex_half(r):
+            sc, off = sc_t[(B - 1, r)]
+            o = outp.tile([P, 2, P], F32, name="oh", tag="oh", bufs=2)
+            nc.vector.scalar_tensor_tensor(
+                out=o[:, r, :], in0=sc[:], scalar=bias[:, 0:1], in1=dmask[:, 0:P], op0=ADD, op1=MULT
+            )
+            nc.scalar.activation(out=o[:, 1 - r, :], in_=off[:], func=IDENTITY, bias=bias[:, 0:1])
             nc.sync.dma_start(
-                out=out[b0 : b0 + nb].rearrange("b (p r) j -> p b (r j)", r=2), in_=o[:]
+                out=out[B - 1][P * r : P * (r + 1), :], in_=o[:].rearrange("p h j -> p (h j)")
+            )
+
+        def store_blocks(bb, o, k):
+            nc.sync.dma_start(
+                out=out[bb].rearrange("(r p) j -> p r j", r=2),
+                in_=o[:, k, :].rearrange("p (r j) -> p r j", r=2),
+            )
+
+        def store(b0, nb, o, k):
+            nc.sync.dma_start(
+                out=out[b0 : b0 + nb].rearrange("b (p r) j -> p b (r j)", r=2), in_=o[:, k : k + nb, :]
             )
 
         def ex(c, j):
@@ -292,10 +340,7 @@ def tile_readingorderhead_t_kernel(tc, panel_embeddings, W, b, out):
                 nc.scalar.activation(
                     out=o4[:, 1:3, :], in_=off[:, 0:2, :], func=IDENTITY, bias=bias[:, 0:1]
                 )
-                if c == NC - 1:
-                    store(bb, 1, o, True)
-                elif j == 1:
-                    store(bb - 1, 2, o, True)
+                store_blocks(bb, o, k)
                 return
             nc.vector.scalar_tensor_tensor(
                 out=o[:, k, :],
@@ -305,10 +350,10 @@ def tile_readingorderhead_t_kernel(tc, panel_embeddings, W, b, out):
                 op0=ADD,
                 op1=MULT,
             )
-            if c == NC - 1:
-                store(bb, 1, o)
+            if c == SPLIT_FROM - 1:
+                store(bb, 1, o, k)
             elif j == 1:
-                store(bb - 1, 2, o)
+                store(bb - 1, 2, o, 0)
                 if c + LOADS_AHEAD < NC:
                     load_x(2 * (c + LOADS_AHEAD), 2)
 
@@ -337,20 +382,15 @@ def tile_readingorderhead_t_kernel(tc, panel_embeddings, W, b, out):
         tr(2)
         qx(1)
         cw(0, 2)
-        for i in range(1, NC + 2):
+        for i in range(1, NC):
             s1(i, 0)
             cw(i - 1, 3, i==2)
             s1(i, 1)
             cx(i + 1, 0)
             s1(i, 2)
             s1(i, 3)
-            if i == NC:
-                qw_batch(B - 2)
-                ex(i - 2, 0)
-                qw_batch(B - 1)
-            else:
-                ex(i - 2, 0)
-                qw(i - 1)
+            ex(i - 2, 0)
+            qw(i - 1)
             cx(i + 1, 1, i == 1)
             ex(i - 2, 1)
             tr(i + 2)
@@ -359,3 +399,16 @@ def tile_readingorderhead_t_kernel(tc, panel_embeddings, W, b, out):
             qx(i + 1)
             cw(i, 1, 1 < i < 14 and i % 6 != 0)
             cw(i, 2)
+
+        qw_batch(B - 2)
+        ex(NC - 2, 0)
+        cw(NC - 1, 3)
+        ex(NC - 2, 1)
+        qw_half(0)
+        s2(NC - 1)
+        s2_half(0)
+        qw_half(1)
+        s2_half(1)
+        ex(NC - 1, 0)
+        ex_half(0)
+        ex_half(1)

@@ -61,7 +61,7 @@ def tile_readingorderhead_t_kernel(tc, panel_embeddings, W, b, out):
         nc.scalar.dma_start(out=b_row[0:1, 0:1], in_=b.unsqueeze(0))
         ones = const.tile([P, P], BF16, name="ones")
         nc.vector.memset(ones[:], 1.0)
-        zeros = const.tile([P, 512], BF16, name="zeros")
+        zeros = const.tile([P, 256], F32, name="zeros")
         nc.vector.memset(zeros[:], 0.0)
         for c in range(1, LOADS_AHEAD):
             load_x(2 * c, 2)
@@ -82,19 +82,15 @@ def tile_readingorderhead_t_kernel(tc, panel_embeddings, W, b, out):
             )
         bias = const.tile([P, 1], F32, name="bias")
 
-        wg = const.tile([P, 4 * D], BF16, name="wg", align_bytes=64)
-        wc = const.tile([P, D], U32, name="wc", align_bytes=64)
-        ws = const.tile([P, D], U8, name="ws", align_bytes=64)
+        wg = const.tile([P, 4 * D], BF16, name="wg", align_bytes=256)
+        wc = const.tile([P, D], U32, name="wc", align_bytes=256)
+        ws = const.tile([P, D], U8, name="ws", align_bytes=256)
 
         def w_regroup():
-            wg_v = wg[:].rearrange("p (o m t) -> p o m t", o=4, m=P, t=4)
-            w_v = w_raw[:].rearrange("p t (m o) -> p o m t", m=P, o=4)
+            wg_v = wg[:].rearrange("p (o c i t) -> p o c t i", o=4, i=4, t=4)
+            w_v = w_raw[:].rearrange("p t (c i o) -> p o c t i", i=4, o=4)
             for o in range(4):
-                src = w_v[:, o, :, :]
-                if o == 3:
-                    nc.scalar.copy(out=wg_v[:, o, :, :], in_=src)
-                else:
-                    nc.vector.tensor_copy(out=wg_v[:, o, :, :], in_=src)
+                copy_out(o < 3, wg_v[:, o, :, :, :], w_v[:, o, :, :, :])
 
         def w_quantise():
             nc.vector.quantize_mx(out=wc[:].bitcast(FP8X4), scales=ws[:], in_=wg[:])
@@ -121,7 +117,7 @@ def tile_readingorderhead_t_kernel(tc, panel_embeddings, W, b, out):
         def warm(n):
             wp = psum.tile([P, 512], F32, name="wp", tag="xw", bufs=4)
             for k in range(n):
-                nc.tensor.matmul(out=wp[:], lhsT=ones[:], rhs=zeros[:], start=True, stop=True)
+                nc.tensor.matmul(out=wp[:], lhsT=ones[:], rhs=zeros[:].bitcast(BF16), start=True, stop=True)
 
         def tr_batch(bb):
             xr, j = x_of[bb]
@@ -142,10 +138,10 @@ def tile_readingorderhead_t_kernel(tc, panel_embeddings, W, b, out):
                 return
             bb = 2 * c + j
             if c == 0:
-                xg = work.tile([P, 4 * N], BF16, name="xg", tag="xg", align_bytes=64)
+                xg = work.tile([P, 4 * N], BF16, name="xg", tag="xg", align_bytes=256)
                 xg_of[bb] = (xg, 0)
             elif j == 0:
-                xg = work.tile([P, 8 * N], BF16, name="xg", tag="xg", align_bytes=64)
+                xg = work.tile([P, 8 * N], BF16, name="xg", tag="xg", align_bytes=256)
                 xg_of[bb] = (xg, 0)
                 xg_of[bb + 1] = (xg, 1)
             xg, k = xg_of[bb]
@@ -153,8 +149,8 @@ def tile_readingorderhead_t_kernel(tc, panel_embeddings, W, b, out):
             copy_out(on_vector, dst, xt_t[bb][:].rearrange("q s p -> q p s"))
 
         def quantise(src, nb, tag, bufs):
-            cod = work.tile([P, nb * N], U32, name=tag + "c", tag=tag + "c", bufs=bufs, align_bytes=64)
-            sca = work.tile([P, nb * N], U8, name=tag + "s", tag=tag + "s", bufs=bufs, align_bytes=64)
+            cod = work.tile([P, nb * N], U32, name=tag + "c", tag=tag + "c", bufs=bufs, align_bytes=256)
+            sca = work.tile([P, nb * N], U8, name=tag + "s", tag=tag + "s", bufs=bufs, align_bytes=256)
             nc.vector.quantize_mx(out=cod[:].bitcast(FP8X4), scales=sca[:], in_=src[:])
             return cod, sca
 
@@ -192,10 +188,10 @@ def tile_readingorderhead_t_kernel(tc, panel_embeddings, W, b, out):
             bb, a = 2 * c + g // 2, g % 2
             if c == NC - 1:
                 if a == 0:
-                    xwg = work.tile([P, 4 * N], BF16, name="xwg", tag="xwg", align_bytes=64)
+                    xwg = work.tile([P, 4 * N], BF16, name="xwg", tag="xwg", align_bytes=256)
                     xwg_of[bb] = (xwg, 0, 1)
             elif g == 0:
-                xwg = work.tile([P, 8 * N], BF16, name="xwg", tag="xwg", align_bytes=64)
+                xwg = work.tile([P, 8 * N], BF16, name="xwg", tag="xwg", align_bytes=256)
                 xwg_of[bb] = (xwg, 0, 2)
                 xwg_of[bb + 1] = (xwg, 1, 2)
             xwg, k, nb = xwg_of[bb]
@@ -262,8 +258,8 @@ def tile_readingorderhead_t_kernel(tc, panel_embeddings, W, b, out):
                 sc_t[bb] = sc
 
         def qw_half(a):
-            cod = work.tile([P, P], U32, name="whc", tag="whc", bufs=2, align_bytes=64)
-            sca = work.tile([P, P], U8, name="whs", tag="whs", bufs=2, align_bytes=64)
+            cod = work.tile([P, P], U32, name="whc", tag="whc", bufs=2, align_bytes=256)
+            sca = work.tile([P, P], U8, name="whs", tag="whs", bufs=2, align_bytes=256)
             xwg = xwg_of[B - 1][0]
             nc.vector.quantize_mx(
                 out=cod[:].bitcast(FP8X4), scales=sca[:], in_=xwg[:, 4 * P * a : 4 * P * (a + 1)]
@@ -359,12 +355,12 @@ def tile_readingorderhead_t_kernel(tc, panel_embeddings, W, b, out):
 
         warm(3)
         tr_batch(0)
-        warm(2)
+        warm(3)
         cx(0, 0)
         w_regroup()
         spread_bias()
         tr_batch(1)
-        warm(1)
+        warm(2)
         qx_batch(0)
         w_quantise()
         cx(0, 1)

from contextlib import ExitStack

import concourse.mybir as mybir
from concourse.masks import make_identity

F32 = mybir.dt.float32
BF16 = mybir.dt.bfloat16
U32 = mybir.dt.uint32
U8 = mybir.dt.uint8
FP8X4 = mybir.dt.float8_e4m3fn_x4
ADD = mybir.AluOpType.add
MULT = mybir.AluOpType.mult
IDENTITY = mybir.ActivationFunctionType.Identity
SPLIT_FROM = 14

P = 128
B, N, D = 32, 256, 512
FLOPS = 2 * B * N * D * D + 2 * B * N * N * D
NC = B // 2
MANUAL = True
LOADS_AHEAD = 10
XQ_BUFS = 16
WQ_BUFS = 16


def tile_readingorderhead_t_kernel(tc, panel_embeddings, W, b, out):
    nc = tc.nc
    x = panel_embeddings
    with ExitStack() as ctx:
        const = ctx.enter_context(tc.tile_pool(name="const", bufs=1))
        xin = ctx.enter_context(tc.tile_pool(name="xin", bufs=1))
        work = ctx.enter_context(tc.tile_pool(name="work", bufs=3))
        outp = ctx.enter_context(tc.tile_pool(name="outp", bufs=16))
        psum = ctx.enter_context(tc.psum_pool(name="psum", bufs=2))
        if MANUAL:
            ctx.enter_context(tc.manual_schedule())

        x_of = {}

        def load_x(b0, nb):
            if nb == 1:
                xr = xin.tile([P, 2 * D], BF16, name="x_raw%d" % b0)
            else:
                xr = xin.tile([P, 4 * D], BF16, name="x_raw", tag="x_raw", bufs=LOADS_AHEAD)
            nc.sync.dma_start(
                out=xr[:].rearrange("p (b f) -> p b f", b=nb),
                in_=x[b0 : b0 + nb].rearrange("b (p r) d -> p b (r d)", r=2),
            )
            for j in range(nb):
                x_of[b0 + j] = (xr, j)

        load_x(0, 1)
        w_raw = const.tile([P, 4, D], BF16, name="w_raw")
        nc.sync.dma_start(
            out=w_raw[:].rearrange("p t n -> p (t n)"),
            in_=W.rearrange("(p t) n -> p (t n)", t=4),
        )
        load_x(1, 1)
        b_row = const.tile([P, 32], BF16, name="b_row")
        nc.vector.memset(b_row[:], 0.0)
        nc.scalar.dma_start(out=b_row[0:1, 0:1], in_=b.unsqueeze(0))
        ones = const.tile([P, P], BF16, name="ones")
        nc.vector.memset(ones[:], 1.0)
        zeros = const.tile([P, 256], F32, name="zeros")
        nc.vector.memset(zeros[:], 0.0)
        for c in range(1, LOADS_AHEAD):
            load_x(2 * c, 2)

        ident = const.tile([P, P], F32, name="ident")
        make_identity(nc, ident[:])
        mask = const.tile([P, 2 * N], F32, name="mask")
        nc.vector.memset(mask[:], 1.0)
        mask_v = mask[:].rearrange("p (r q s) -> p r q s", r=2, q=P, s=2)
        for r in range(2):
            nc.vector.tensor_scalar(
                out=mask_v[:, r, :, r], in0=ident[:], scalar1=-1.0, scalar2=1.0, op0=MULT, op1=ADD
            )
        dmask = const.tile([P, 2 * P], F32, name="dmask")
        for r in range(2):
            nc.vector.tensor_scalar(
                out=dmask[:, P * r : P * (r + 1)], in0=ident[:], scalar1=-1.0, scalar2=1.0, op0=MULT, op1=ADD
            )
        bias = const.tile([P, 1], F32, name="bias")

        wg = const.tile([P, 4 * D], BF16, name="wg", align_bytes=256)
        wc = const.tile([P, D], U32, name="wc", align_bytes=256)
        ws = const.tile([P, D], U8, name="ws", align_bytes=256)

        def w_regroup():
            wg_v = wg[:].rearrange("p (o c i t) -> p o c t i", o=4, i=4, t=4)
            w_v = w_raw[:].rearrange("p t (c i o) -> p o c t i", i=4, o=4)
            for o in range(4):
                copy_out(o < 3, wg_v[:, o, :, :, :], w_v[:, o, :, :, :])

        def w_quantise():
            nc.vector.quantize_mx(out=wc[:].bitcast(FP8X4), scales=ws[:], in_=wg[:])
            nc.vector.tensor_copy(out=bias[:], in_=bias_ps[0][:, 0:1])

        xt_t, xg_of, xc_of, xw_t, xwg_of, xwc_of, sc_t, o_of = {}, {}, {}, {}, {}, {}, {}, {}

        def ok(c):
            return 0 <= c < NC

        def copy_out(on_vector, dst, src):
            if on_vector:
                nc.vector.tensor_copy(out=dst, in_=src)
            else:
                nc.scalar.copy(out=dst, in_=src)

        bias_ps = []

        def spread_bias():
            bp = psum.tile([P, 32], F32, name="bp", tag="sc", bufs=2)
            nc.tensor.matmul(out=bp[:], lhsT=ones[:], rhs=b_row[:], start=True, stop=True)
            bias_ps.append(bp)

        def warm(n):
            wp = psum.tile([P, 512], F32, name="wp", tag="xw", bufs=4)
            for k in range(n):
                nc.tensor.matmul(out=wp[:], lhsT=ones[:], rhs=zeros[:].bitcast(BF16), start=True, stop=True)

        def tr_batch(bb):
            xr, j = x_of[bb]
            xr32 = xr[:].bitcast(F32)
            xt = psum.tile([P, 4, P], F32, name="xt", tag="xt", bufs=2)
            for s in range(4):
                lo = 512 * j + 256 * (s // 2)
                nc.tensor.transpose(xt[:, s, :], xr32[:, lo + s % 2 : lo + 256 : 2], ident[:])
            xt_t[bb] = xt

        def tr(c):
            if ok(c):
                tr_batch(2 * c)
                tr_batch(2 * c + 1)

        def cx(c, j, on_vector=False):
            if not ok(c):
                return
            bb = 2 * c + j
            if c == 0:
                xg = work.tile([P, 4 * N], BF16, name="xg", tag="xg", align_bytes=256)
                xg_of[bb] = (xg, 0)
            elif j == 0:
                xg = work.tile([P, 8 * N], BF16, name="xg", tag="xg", align_bytes=256)
                xg_of[bb] = (xg, 0)
                xg_of[bb + 1] = (xg, 1)
            xg, k = xg_of[bb]
            dst = xg[:].bitcast(F32)[:, 512 * k : 512 * (k + 1)].rearrange("q (p s) -> q p s", s=4)
            copy_out(on_vector, dst, xt_t[bb][:].rearrange("q s p -> q p s"))

        def quantise(src, nb, tag, bufs):
            cod = work.tile([P, nb * N], U32, name=tag + "c", tag=tag + "c", bufs=bufs, align_bytes=256)
            sca = work.tile([P, nb * N], U8, name=tag + "s", tag=tag + "s", bufs=bufs, align_bytes=256)
            nc.vector.quantize_mx(out=cod[:].bitcast(FP8X4), scales=sca[:], in_=src[:])
            return cod, sca

        def qx_batch(bb):
            cod, sca = quantise(xg_of[bb][0], 1, "xq", XQ_BUFS)
            xc_of[bb] = (cod, sca, 0)

        def qx(c):
            if ok(c):
                cod, sca = quantise(xg_of[2 * c][0], 2, "xq", XQ_BUFS)
                xc_of[2 * c] = (cod, sca, 0)
                xc_of[2 * c + 1] = (cod, sca, 1)

        def s1(c, g):
            if not ok(c):
                return
            cod, sca, k = xc_of[2 * c + g // 2]
            lo = N * k + P * (g % 2)
            xw = psum.tile([P, 4, P], F32, name="xw", tag="xw", bufs=4)
            for t in range(4):
                nc.tensor.matmul_mx(
                    out=xw[:, t, :],
                    lhsT=wc[:, P * t : P * (t + 1)].bitcast(FP8X4),
                    lhsT_scale=ws[:, P * t : P * (t + 1)],
                    rhs=cod[:, lo : lo + P].bitcast(FP8X4),
                    rhs_scale=sca[:, lo : lo + P],
                    start=True,
                    stop=True,
                )
            xw_t[(c, g)] = xw

        def cw(c, g, on_vector=False):
            if not ok(c):
                return
            bb, a = 2 * c + g // 2, g % 2
            if c == NC - 1:
                if a == 0:
                    xwg = work.tile([P, 4 * N], BF16, name="xwg", tag="xwg", align_bytes=256)
                    xwg_of[bb] = (xwg, 0, 1)
            elif g == 0:
                xwg = work.tile([P, 8 * N], BF16, name="xwg", tag="xwg", align_bytes=256)
                xwg_of[bb] = (xwg, 0, 2)
                xwg_of[bb + 1] = (xwg, 1, 2)
            xwg, k, nb = xwg_of[bb]
            xwg_v = xwg[:].rearrange("p (b r m t) -> p b r m t", b=nb, r=2, m=P, t=4)
            if c >= SPLIT_FROM:
                dst = xwg[:].rearrange("p (n t) -> p n t", t=4)[:, N * k + P * a : N * k + P * (a + 1), :]
                src = xw_t[(c, g)][:].rearrange("p t n -> p n t")
            else:
                dst = xwg_v[:, k, :, 64 * a : 64 * (a + 1), :]
                src = xw_t[(c, g)][:].rearrange("p t (m r) -> p r m t", r=2)
            copy_out(on_vector, dst, src)

        def qw_batch(bb):
            cod, sca = quantise(xwg_of[bb][0], 1, "wq", WQ_BUFS)
            xwc_of[bb] = (cod, sca, 0)

        def qw(c):
            if not ok(c):
                return
            cod, sca = quantise(xwg_of[2 * c][0], 2, "wq", WQ_BUFS)
            xwc_of[2 * c] = (cod, sca, 0)
            xwc_of[2 * c + 1] = (cod, sca, 1)

        def s2(c):
            if not ok(c):
                return
            for bb in (2 * c, 2 * c + 1):
                if bb == B - 1:
                    continue
                xcod, xsca, k = xc_of[bb]
                wcod, wsca, kw = xwc_of[bb]
                sc = psum.tile([P, 2, N], F32, name="sc", tag="sc", bufs=2)
                if c >= SPLIT_FROM:
                    if c == NC - 1:
                        off = psum.tile([P, 4, P], F32, name="off", tag="xw", bufs=4)
                    else:
                        off = psum.tile([P, 4, P], F32, name="off", tag="xt", bufs=2)
                    for r in range(2):
                        lo = N * kw + P * r
                        for h in range(2):
                            hi = N * k + P * h
                            nc.tensor.matmul_mx(
                                out=(sc[:, 0, P * r : P * (r + 1)] if h == r else off[:, r, :]),
                                lhsT=wcod[:, lo : lo + P].bitcast(FP8X4),
                                lhsT_scale=wsca[:, lo : lo + P],
                                rhs=xcod[:, hi : hi + P].bitcast(FP8X4),
                                rhs_scale=xsca[:, hi : hi + P],
                                start=True,
                                stop=True,
                            )
                    sc_t[bb] = (sc, off)
                    continue
                for r in range(2):
                    lo = N * kw + P * r
                    nc.tensor.matmul_mx(
                        out=sc[:, r, :],
                        lhsT=wcod[:, lo : lo + P].bitcast(FP8X4),
                        lhsT_scale=wsca[:, lo : lo + P],
                        rhs=xcod[:, N * k : N * (k + 1)].bitcast(FP8X4),
                        rhs_scale=xsca[:, N * k : N * (k + 1)],
                        start=True,
                        stop=True,
                    )
                sc_t[bb] = sc

        def qw_half(a):
            cod = work.tile([P, P], U32, name="whc", tag="whc", bufs=2, align_bytes=256)
            sca = work.tile([P, P], U8, name="whs", tag="whs", bufs=2, align_bytes=256)
            xwg = xwg_of[B - 1][0]
            nc.vector.quantize_mx(
                out=cod[:].bitcast(FP8X4), scales=sca[:], in_=xwg[:, 4 * P * a : 4 * P * (a + 1)]
            )
            xwc_of[(B - 1, a)] = (cod, sca)

        def s2_half(r):
            xcod, xsca, k = xc_of[B - 1]
            wcod, wsca = xwc_of[(B - 1, r)]
            if r == 0:
                sc = psum.tile([P, P], F32, name="sch0", tag="sc", bufs=2)
                off = psum.tile([P, P], F32, name="offh0", tag="xt", bufs=2)
            else:
                sc = psum.tile([P, P], F32, name="sch1", tag="xw", bufs=4)
                off = psum.tile([P, P], F32, name="offh1", tag="xw", bufs=4)
            for h in range(2):
                hi = N * k + P * h
                nc.tensor.matmul_mx(
                    out=sc[:] if h == r else off[:],
                    lhsT=wcod[:].bitcast(FP8X4),
                    lhsT_scale=wsca[:],
                    rhs=xcod[:, hi : hi + P].bitcast(FP8X4),
                    rhs_scale=xsca[:, hi : hi + P],
                    start=True,
                    stop=True,
                )
            sc_t[(B - 1, r)] = (sc, off)

        def ex_half(r):
            sc, off = sc_t[(B - 1, r)]
            o = outp.tile([P, 2, P], F32, name="oh", tag="oh", bufs=2)
            nc.vector.scalar_tensor_tensor(
                out=o[:, r, :], in0=sc[:], scalar=bias[:, 0:1], in1=dmask[:, 0:P], op0=ADD, op1=MULT
            )
            nc.scalar.activation(out=o[:, 1 - r, :], in_=off[:], func=IDENTITY, bias=bias[:, 0:1])
            nc.sync.dma_start(
                out=out[B - 1][P * r : P * (r + 1), :], in_=o[:].rearrange("p h j -> p (h j)")
            )

        def store_blocks(bb, o, k):
            nc.sync.dma_start(
                out=out[bb].rearrange("(r p) j -> p r j", r=2),
                in_=o[:, k, :].rearrange("p (r j) -> p r j", r=2),
            )

        def store(b0, nb, o, k):
            nc.sync.dma_start(
                out=out[b0 : b0 + nb].rearrange("b (p r) j -> p b (r j)", r=2), in_=o[:, k : k + nb, :]
            )

        def ex(c, j):
            if not ok(c):
                return
            bb = 2 * c + j
            if c == NC - 1:
                o = outp.tile([P, 1, 2 * N], F32, name="o", tag="o")
                o_of[bb] = (o, 0)
            elif j == 0:
                o = outp.tile([P, 2, 2 * N], F32, name="o", tag="o")
                o_of[bb] = (o, 0)
                o_of[bb + 1] = (o, 1)
            o, k = o_of[bb]
            if c >= SPLIT_FROM:
                sc, off = sc_t[bb]
                o4 = o[:, k, :].rearrange("p (g j) -> p g j", g=4)
                nc.vector.scalar_tensor_tensor(
                    out=o4[:, 0:4:3, :],
                    in0=sc[:, 0, :].rearrange("p (r j) -> p r j", r=2),
                    scalar=bias[:, 0:1],
                    in1=dmask[:].rearrange("p (r j) -> p r j", r=2),
                    op0=ADD,
                    op1=MULT,
                )
                nc.scalar.activation(
                    out=o4[:, 1:3, :], in_=off[:, 0:2, :], func=IDENTITY, bias=bias[:, 0:1]
                )
                store_blocks(bb, o, k)
                return
            nc.vector.scalar_tensor_tensor(
                out=o[:, k, :],
                in0=sc_t[bb][:].rearrange("p r j -> p (r j)"),
                scalar=bias[:, 0:1],
                in1=mask[:],
                op0=ADD,
                op1=MULT,
            )
            if c == SPLIT_FROM - 1:
                store(bb, 1, o, k)
            elif j == 1:
                store(bb - 1, 2, o, 0)
                if c + LOADS_AHEAD < NC:
                    load_x(2 * (c + LOADS_AHEAD), 2)

        warm(3)
        tr_batch(0)
        warm(3)
        cx(0, 0)
        w_regroup()
        spread_bias()
        tr_batch(1)
        warm(2)
        qx_batch(0)
        w_quantise()
        cx(0, 1)
        qx_batch(1)
        tr_batch(2)
        s1(0, 0)
        s1(0, 1)
        cx(1, 0)
        cw(0, 0, True)
        tr_batch(3)
        cw(0, 1)
        s1(0, 2)
        s1(0, 3)
        cx(1, 1, True)
        tr(2)
        qx(1)
        cw(0, 2)
        for i in range(1, NC):
            s1(i, 0)
            cw(i - 1, 3, i==2)
            s1(i, 1)
            cx(i + 1, 0)
            s1(i, 2)
            s1(i, 3)
            ex(i - 2, 0)
            qw(i - 1)
            cx(i + 1, 1, i == 1)
            ex(i - 2, 1)
            tr(i + 2)
            cw(i, 0)
            s2(i - 1)
            qx(i + 1)
            cw(i, 1, 1 < i < 14 and i % 6 != 0)
            cw(i, 2)

        qw_batch(B - 2)
        ex(NC - 2, 0)
        cw(NC - 1, 3)
        ex(NC - 2, 1)
        qw_half(0)
        s2(NC - 1)
        s2_half(0)
        qw_half(1)
        s2_half(1)
        ex(NC - 1, 0)
        ex_half(0)
        ex_half(1)
